import numpy as np
import ml_dtypes

BF16 = ml_dtypes.bfloat16


def bf(x):
    return np.asarray(x, np.float32).astype(BF16)


def f32(x):
    return np.asarray(x, np.float32)


def f64(x):
    return np.asarray(x).astype(np.float64)


def striped(idx):
    return np.tile(idx.reshape(-1, 16).T, (8, 1))


D, S, N, DM = 128, 512, 512, 512
TANH_CLIP = 10.0


def setup_inputs():
    return {"table": bf(np.random.standard_normal((D, S))), "w": bf(2.0 * np.random.standard_normal((D, S))), "vals": bf(np.random.standard_normal((S, D))), "lkeys": bf(2.0 * np.random.standard_normal((D, S))), "offs": striped(np.random.permutation(np.tile(np.arange(S), 2))[:N])}


def reference(table, w, vals, lkeys, offs):
    idx = offs[:16].T.reshape(-1)
    sc = f64(w).T @ f64(table)[:, idx] / np.sqrt(D)
    e = np.exp(sc - sc.max(axis=0, keepdims=True))
    a = e / e.sum(axis=0, keepdims=True)
    h = f64(vals).T @ a
    u = TANH_CLIP * np.tanh(f64(lkeys).T @ h / np.sqrt(DM))
    return u - np.log(np.exp(u).sum(axis=0, keepdims=True))

@@ -1,0 +1,134 @@
+import math
+
+import concourse.mybir as mybir
+from concourse.masks import make_identity
+
+BF16 = mybir.dt.bfloat16
+F32 = mybir.dt.float32
+U16 = mybir.dt.uint16
+FUNC = mybir.ActivationFunctionType
+ALU = mybir.AluOpType
+AXIS = mybir.AxisListType
+
+P = 128
+D = 128
+NODES = 512
+STEPS = 512
+POINTER_DIM = 512
+TANH_CLIP = 10.0
+NB = NODES // P
+CHUNK = 128
+NCHUNK = STEPS // CHUNK
+OFFSETS_PER_COLUMN = 16
+CHUNK_COLUMNS = CHUNK // OFFSETS_PER_COLUMN
+ONES_PAD = 16
+
+FLOPS = 3 * 2 * D * NODES * STEPS
+
+
+def tile_autoregressivedecoder_kernel(tc, table, w, vals, lkeys, offs, out):
+    nc = tc.nc
+    with (
+        tc.tile_pool(name="held", bufs=1) as held,
+        tc.tile_pool(name="work", bufs=2) as work,
+        tc.psum_pool(name="wide", bufs=NCHUNK) as wide,
+        tc.psum_pool(name="narrow", bufs=1) as narrow,
+    ):
+        offsets = held.tile([P, STEPS // OFFSETS_PER_COLUMN], U16, name="offsets")
+        nc.sync.dma_start(offsets[:], offs)
+        table_sb = held.tile([D, NODES], BF16, name="table_sb")
+        nc.sync.dma_start(table_sb[:], table)
+        keys_sb = held.tile([D, NODES], BF16, name="keys_sb")
+        nc.scalar.dma_start(keys_sb[:], w)
+        values_sb = held.tile([P, NB, D + ONES_PAD], BF16, name="values_sb")
+        nc.sync.dma_start(values_sb[:, :, 0:D], vals.rearrange("(b p) d -> p b d", p=P))
+        nc.vector.memset(values_sb[:, :, D : D + ONES_PAD], 1.0)
+        pointer_sb = held.tile([D, NODES], BF16, name="pointer_sb")
+        nc.scalar.dma_start(pointer_sb[:], lkeys)
+
+        ident_f32 = held.tile([P, P], F32, name="ident_f32")
+        make_identity(nc, ident_f32[:])
+        ident_bf16 = held.tile([P, P], BF16, name="ident_bf16")
+        make_identity(nc, ident_bf16[:])
+        ones_f32 = held.tile([P, P], F32, name="ones_f32")
+        nc.vector.memset(ones_f32[:], 1.0)
+        zeros_f32 = held.tile([P, P], F32, name="zeros_f32")
+        nc.vector.memset(zeros_f32[:], 0.0)
+
+        clipped = held.tile([P, NCHUNK, NB, CHUNK], F32, name="clipped")
+        expsum = narrow.tile([P, NCHUNK, CHUNK], F32, name="expsum")
+        logsum = held.tile([P, NCHUNK, CHUNK], F32, name="logsum")
+
+        scores = [wide.tile([P, NB, CHUNK], F32, name="scores", tag="wide") for c in range(NCHUNK)]
+        for c in range(NCHUNK):
+            picked = table_sb[:].indirect(offsets[:, c * CHUNK_COLUMNS : (c + 1) * CHUNK_COLUMNS])
+            for b in range(NB):
+                nc.tensor.matmul(
+                    scores[c][:, b, :], keys_sb[:, b * P : (b + 1) * P], picked, start=True, stop=True
+                )
+
+        for c in range(NCHUNK):
+            block_top = work.tile([P, CHUNK], F32, name="block_top")
+            nc.vector.tensor_reduce(
+                out=block_top[:], in_=scores[c][:].rearrange("n b j -> n j b"), axis=AXIS.X, op=ALU.max
+            )
+            turned = narrow.tile([P, 2, P], F32, name="turned")
+            nc.tensor.transpose(turned[:, 0, :], block_top[:], ident_f32[:])
+            top = work.tile([CHUNK, 1], F32, name="top")
+            nc.vector.reduce_max(out=top[:], in_=turned[:, 0, :], axis=AXIS.X)
+            top_repeated = work.tile([CHUNK, P], F32, name="top_repeated")
+            nc.vector.tensor_scalar(
+                out=top_repeated[:], in0=zeros_f32[:], scalar1=top[:, 0:1], scalar2=None, op0=ALU.add
+            )
+            nc.tensor.transpose(turned[:, 1, :], top_repeated[:], ident_f32[:])
+            top_row = work.tile([P, CHUNK], F32, name="top_row")
+            nc.scalar.copy(top_row[:], turned[:, 1, :])
+
+            shifted = work.tile([P, NB, CHUNK], F32, name="shifted")
+            nc.vector.tensor_tensor(
+                out=shifted[:],
+                in0=scores[c][:],
+                in1=top_row[:].unsqueeze(1).to_broadcast([P, NB, CHUNK]),
+                op=ALU.subtract,
+            )
+            weights = work.tile([P, NB, CHUNK], BF16, name="weights")
+            nc.scalar.activation(out=weights[:], in_=shifted[:], func=FUNC.Exp, scale=1.0 / math.sqrt(D))
+
+            glimpse_t = narrow.tile([CHUNK, D + 1], F32, name="glimpse_t")
+            for b in range(NB):
+                nc.tensor.matmul(
+                    glimpse_t[:], weights[:, b, :], values_sb[:, b, 0 : D + 1], start=(b == 0), stop=(b == NB - 1)
+                )
+            inv_sum = work.tile([CHUNK, 1], F32, name="inv_sum")
+            nc.vector.reciprocal(inv_sum[:], glimpse_t[:, D : D + 1])
+            glimpse_rows = work.tile([CHUNK, D], BF16, name="glimpse_rows")
+            nc.scalar.activation(out=glimpse_rows[:], in_=glimpse_t[:, 0:D], func=FUNC.Copy, scale=inv_sum[:, 0:1])
+            glimpse_ps = narrow.tile([D, CHUNK], BF16, name="glimpse_ps")
+            nc.tensor.transpose(glimpse_ps[:], glimpse_rows[:], ident_bf16[:])
+            glimpse = work.tile([D, CHUNK], BF16, name="glimpse")
+            nc.vector.tensor_copy(glimpse[:], glimpse_ps[:])
+
+            logits = wide.tile([P, NB, CHUNK], F32, name="logits", tag="wide")
+            for b in range(NB):
+                nc.tensor.matmul(logits[:, b, :], pointer_sb[:, b * P : (b + 1) * P], glimpse[:], start=True, stop=True)
+            nc.scalar.activation(
+                out=clipped[:, c], in_=logits[:], func=FUNC.Tanh, scale=1.0 / math.sqrt(POINTER_DIM)
+            )
+            grown = work.tile([P, NB, CHUNK], F32, name="grown")
+            nc.scalar.activation(out=grown[:], in_=clipped[:, c], func=FUNC.Exp, scale=TANH_CLIP)
+            for b in range(NB):
+                nc.tensor.matmul(expsum[:, c, :], ones_f32[:], grown[:, b, :], start=(b == 0), stop=(b == NB - 1))
+
+        nc.scalar.activation(out=logsum[:], in_=expsum[:], func=FUNC.Ln)
+        out_blocks = out.rearrange("(b n) j -> n b j", n=P)
+        for c in range(NCHUNK):
+            logprob = work.tile([P, NB, CHUNK], F32, name="logprob")
+            nc.vector.scalar_tensor_tensor(
+                out=logprob[:],
+                in0=clipped[:, c],
+                scalar=TANH_CLIP,
+                in1=logsum[:, c, :].unsqueeze(1).to_broadcast([P, NB, CHUNK]),
+                op0=ALU.mult,
+                op1=ALU.subtract,
+            )
+            nc.sync.dma_start(out_blocks[:, :, c * CHUNK : (c + 1) * CHUNK], logprob[:])

@@ -30,16 +30,17 @@ def tile_autoregressivedecoder_kernel(tc, table, w, vals, lkeys, offs, out):
     nc = tc.nc
     with (
         tc.tile_pool(name="held", bufs=1) as held,
-        tc.tile_pool(name="work", bufs=2) as work,
-        tc.psum_pool(name="wide", bufs=NCHUNK) as wide,
-        tc.psum_pool(name="narrow", bufs=1) as narrow,
+        tc.tile_pool(name="work", bufs=NCHUNK) as work,
+        tc.psum_pool(name="psum_wide", bufs=3) as psum_wide,
+        tc.psum_pool(name="psum_narrow", bufs=2) as psum_narrow,
+        tc.psum_pool(name="psum_held", bufs=1) as psum_held,
     ):
         offsets = held.tile([P, STEPS // OFFSETS_PER_COLUMN], U16, name="offsets")
         nc.sync.dma_start(offsets[:], offs)
         table_sb = held.tile([D, NODES], BF16, name="table_sb")
-        nc.sync.dma_start(table_sb[:], table)
+        nc.scalar.dma_start(table_sb[:], table)
         keys_sb = held.tile([D, NODES], BF16, name="keys_sb")
-        nc.scalar.dma_start(keys_sb[:], w)
+        nc.sync.dma_start(keys_sb[:], w)
         values_sb = held.tile([P, NB, D + ONES_PAD], BF16, name="values_sb")
         nc.sync.dma_start(values_sb[:, :, 0:D], vals.rearrange("(b p) d -> p b d", p=P))
         nc.vector.memset(values_sb[:, :, D : D + ONES_PAD], 1.0)
@@ -52,72 +53,72 @@ def tile_autoregressivedecoder_kernel(tc, table, w, vals, lkeys, offs, out):
         make_identity(nc, ident_bf16[:])
         ones_f32 = held.tile([P, P], F32, name="ones_f32")
         nc.vector.memset(ones_f32[:], 1.0)
-        zeros_f32 = held.tile([P, P], F32, name="zeros_f32")
-        nc.vector.memset(zeros_f32[:], 0.0)
 
         clipped = held.tile([P, NCHUNK, NB, CHUNK], F32, name="clipped")
-        expsum = narrow.tile([P, NCHUNK, CHUNK], F32, name="expsum")
+        expsum = psum_held.tile([P, NCHUNK, CHUNK], F32, name="expsum")
         logsum = held.tile([P, NCHUNK, CHUNK], F32, name="logsum")
 
-        scores = [wide.tile([P, NB, CHUNK], F32, name="scores", tag="wide") for c in range(NCHUNK)]
-        for c in range(NCHUNK):
-            picked = table_sb[:].indirect(offsets[:, c * CHUNK_COLUMNS : (c + 1) * CHUNK_COLUMNS])
-            for b in range(NB):
-                nc.tensor.matmul(
-                    scores[c][:, b, :], keys_sb[:, b * P : (b + 1) * P], picked, start=True, stop=True
-                )
+        weights = [work.tile([P, NB, CHUNK], BF16, name="weights") for c in range(NCHUNK)]
+        glimpse = [work.tile([D, CHUNK], BF16, name="glimpse") for c in range(NCHUNK)]
 
         for c in range(NCHUNK):
+            scores = psum_wide.tile([P, NB, CHUNK], F32, name="scores", tag="wide")
+            picked = table_sb[:].indirect(offsets[:, c * CHUNK_COLUMNS : (c + 1) * CHUNK_COLUMNS])
+            for b in range(NB):
+                nc.tensor.matmul(scores[:, b, :], keys_sb[:, b * P : (b + 1) * P], picked, start=True, stop=True)
+
             block_top = work.tile([P, CHUNK], F32, name="block_top")
             nc.vector.tensor_reduce(
-                out=block_top[:], in_=scores[c][:].rearrange("n b j -> n j b"), axis=AXIS.X, op=ALU.max
+                out=block_top[:], in_=scores[:].rearrange("n b j -> n j b"), axis=AXIS.X, op=ALU.max
             )
-            turned = narrow.tile([P, 2, P], F32, name="turned")
-            nc.tensor.transpose(turned[:, 0, :], block_top[:], ident_f32[:])
+            scores_sb = work.tile([P, NB, CHUNK], F32, name="scores_sb")
+            nc.scalar.copy(scores_sb[:], scores[:])
+            block_top_t = psum_narrow.tile([CHUNK, P], F32, name="block_top_t", tag="narrow_a")
+            nc.tensor.transpose(block_top_t[:], block_top[:], ident_f32[:])
             top = work.tile([CHUNK, 1], F32, name="top")
-            nc.vector.reduce_max(out=top[:], in_=turned[:, 0, :], axis=AXIS.X)
-            top_repeated = work.tile([CHUNK, P], F32, name="top_repeated")
-            nc.vector.tensor_scalar(
-                out=top_repeated[:], in0=zeros_f32[:], scalar1=top[:, 0:1], scalar2=None, op0=ALU.add
-            )
-            nc.tensor.transpose(turned[:, 1, :], top_repeated[:], ident_f32[:])
-            top_row = work.tile([P, CHUNK], F32, name="top_row")
-            nc.scalar.copy(top_row[:], turned[:, 1, :])
+            nc.vector.reduce_max(out=top[:], in_=block_top_t[:], axis=AXIS.X)
+            top_row = psum_narrow.tile([P, CHUNK], F32, name="top_row", tag="narrow_b")
+            nc.tensor.transpose(top_row[:], top[:, 0:1].to_broadcast([CHUNK, P]), ident_f32[:])
 
             shifted = work.tile([P, NB, CHUNK], F32, name="shifted")
             nc.vector.tensor_tensor(
                 out=shifted[:],
-                in0=scores[c][:],
+                in0=scores_sb[:],
                 in1=top_row[:].unsqueeze(1).to_broadcast([P, NB, CHUNK]),
                 op=ALU.subtract,
             )
-            weights = work.tile([P, NB, CHUNK], BF16, name="weights")
-            nc.scalar.activation(out=weights[:], in_=shifted[:], func=FUNC.Exp, scale=1.0 / math.sqrt(D))
+            nc.scalar.activation(out=weights[c][:], in_=shifted[:], func=FUNC.Exp, scale=1.0 / math.sqrt(D))
 
-            glimpse_t = narrow.tile([CHUNK, D + 1], F32, name="glimpse_t")
+        for c in range(NCHUNK):
+            glimpse_t = psum_narrow.tile([CHUNK, D + 1], F32, name="glimpse_t", tag="narrow_a")
             for b in range(NB):
                 nc.tensor.matmul(
-                    glimpse_t[:], weights[:, b, :], values_sb[:, b, 0 : D + 1], start=(b == 0), stop=(b == NB - 1)
+                    glimpse_t[:], weights[c][:, b, :], values_sb[:, b, 0 : D + 1], start=(b == 0), stop=(b == NB - 1)
                 )
             inv_sum = work.tile([CHUNK, 1], F32, name="inv_sum")
             nc.vector.reciprocal(inv_sum[:], glimpse_t[:, D : D + 1])
             glimpse_rows = work.tile([CHUNK, D], BF16, name="glimpse_rows")
-            nc.scalar.activation(out=glimpse_rows[:], in_=glimpse_t[:, 0:D], func=FUNC.Copy, scale=inv_sum[:, 0:1])
-            glimpse_ps = narrow.tile([D, CHUNK], BF16, name="glimpse_ps")
+            nc.vector.tensor_scalar(
+                out=glimpse_rows[:], in0=glimpse_t[:, 0:D], scalar1=inv_sum[:, 0:1], scalar2=None, op0=ALU.mult
+            )
+            glimpse_ps = psum_narrow.tile([D, CHUNK], BF16, name="glimpse_ps", tag="narrow_b")
             nc.tensor.transpose(glimpse_ps[:], glimpse_rows[:], ident_bf16[:])
-            glimpse = work.tile([D, CHUNK], BF16, name="glimpse")
-            nc.vector.tensor_copy(glimpse[:], glimpse_ps[:])
+            nc.scalar.copy(glimpse[c][:], glimpse_ps[:])
 
-            logits = wide.tile([P, NB, CHUNK], F32, name="logits", tag="wide")
+        for c in range(NCHUNK):
+            logits = psum_wide.tile([P, NB, CHUNK], F32, name="logits", tag="wide")
             for b in range(NB):
-                nc.tensor.matmul(logits[:, b, :], pointer_sb[:, b * P : (b + 1) * P], glimpse[:], start=True, stop=True)
+                nc.tensor.matmul(logits[:, b, :], pointer_sb[:, b * P : (b + 1) * P], glimpse[c][:], start=True, stop=True)
             nc.scalar.activation(
                 out=clipped[:, c], in_=logits[:], func=FUNC.Tanh, scale=1.0 / math.sqrt(POINTER_DIM)
             )
             grown = work.tile([P, NB, CHUNK], F32, name="grown")
             nc.scalar.activation(out=grown[:], in_=clipped[:, c], func=FUNC.Exp, scale=TANH_CLIP)
-            for b in range(NB):
-                nc.tensor.matmul(expsum[:, c, :], ones_f32[:], grown[:, b, :], start=(b == 0), stop=(b == NB - 1))
+            block_sum = work.tile([P, CHUNK], F32, name="block_sum")
+            nc.vector.tensor_reduce(
+                out=block_sum[:], in_=grown[:].rearrange("n b j -> n j b"), axis=AXIS.X, op=ALU.add
+            )
+            nc.tensor.matmul(expsum[:, c, :], ones_f32[:], block_sum[:], start=True, stop=True)
 
         nc.scalar.activation(out=logsum[:], in_=expsum[:], func=FUNC.Ln)
         out_blocks = out.rearrange("(b n) j -> n b j", n=P)

@@ -21,6 +21,7 @@ CHUNK = 128
 NCHUNK = STEPS // CHUNK
 OFFSETS_PER_COLUMN = 16
 CHUNK_COLUMNS = CHUNK // OFFSETS_PER_COLUMN
+WARM_MATMULS = 3
 ONES_PAD = 16
 
 FLOPS = 3 * 2 * D * NODES * STEPS
@@ -35,6 +36,12 @@ def tile_autoregressivedecoder_kernel(tc, table, w, vals, lkeys, offs, out):
         tc.psum_pool(name="psum_narrow", bufs=2) as psum_narrow,
         tc.psum_pool(name="psum_held", bufs=1) as psum_held,
     ):
+        zeros = held.tile([P, NB * CHUNK], BF16, name="zeros")
+        nc.vector.memset(zeros[:], 0.0)
+        warm = psum_wide.tile([P, NB * CHUNK], F32, name="warm", tag="wide")
+        for i in range(WARM_MATMULS):
+            nc.tensor.matmul(warm[:], zeros[:, 0:P], zeros[:], start=True, stop=True)
+
         offsets = held.tile([P, STEPS // OFFSETS_PER_COLUMN], U16, name="offsets")
         nc.sync.dma_start(offsets[:], offs)
         table_sb = held.tile([D, NODES], BF16, name="table_sb")
@@ -103,7 +110,7 @@ def tile_autoregressivedecoder_kernel(tc, table, w, vals, lkeys, offs, out):
             )
             glimpse_ps = psum_narrow.tile([D, CHUNK], BF16, name="glimpse_ps", tag="narrow_b")
             nc.tensor.transpose(glimpse_ps[:], glimpse_rows[:], ident_bf16[:])
-            nc.scalar.copy(glimpse[c][:], glimpse_ps[:])
+            nc.vector.tensor_copy(glimpse[c][:], glimpse_ps[:])
 
         for c in range(NCHUNK):
             logits = psum_wide.tile([P, NB, CHUNK], F32, name="logits", tag="wide")
@@ -121,15 +128,15 @@ def tile_autoregressivedecoder_kernel(tc, table, w, vals, lkeys, offs, out):
             nc.tensor.matmul(expsum[:, c, :], ones_f32[:], block_sum[:], start=True, stop=True)
 
         nc.scalar.activation(out=logsum[:], in_=expsum[:], func=FUNC.Ln)
-        out_blocks = out.rearrange("(b n) j -> n b j", n=P)
-        for c in range(NCHUNK):
-            logprob = work.tile([P, NB, CHUNK], F32, name="logprob")
+        for b in range(NB):
+            logprob = work.tile([P, NCHUNK, CHUNK], F32, name="logprob")
             nc.vector.scalar_tensor_tensor(
                 out=logprob[:],
-                in0=clipped[:, c],
+                in0=clipped[:, :, b, :],
                 scalar=TANH_CLIP,
-                in1=logsum[:, c, :].unsqueeze(1).to_broadcast([P, NB, CHUNK]),
+                in1=logsum[:],
                 op0=ALU.mult,
                 op1=ALU.subtract,
             )
-            nc.sync.dma_start(out_blocks[:, :, c * CHUNK : (c + 1) * CHUNK], logprob[:])
+            queue = nc.sync if b % 2 == 0 else nc.scalar
+            queue.dma_start(out[b * P : (b + 1) * P, :], logprob[:].rearrange("n c j -> n (c j)"))

@@ -21,7 +21,6 @@ CHUNK = 128
 NCHUNK = STEPS // CHUNK
 OFFSETS_PER_COLUMN = 16
 CHUNK_COLUMNS = CHUNK // OFFSETS_PER_COLUMN
-WARM_MATMULS = 3
 ONES_PAD = 16
 
 FLOPS = 3 * 2 * D * NODES * STEPS
@@ -36,12 +35,6 @@ def tile_autoregressivedecoder_kernel(tc, table, w, vals, lkeys, offs, out):
         tc.psum_pool(name="psum_narrow", bufs=2) as psum_narrow,
         tc.psum_pool(name="psum_held", bufs=1) as psum_held,
     ):
-        zeros = held.tile([P, NB * CHUNK], BF16, name="zeros")
-        nc.vector.memset(zeros[:], 0.0)
-        warm = psum_wide.tile([P, NB * CHUNK], F32, name="warm", tag="wide")
-        for i in range(WARM_MATMULS):
-            nc.tensor.matmul(warm[:], zeros[:, 0:P], zeros[:], start=True, stop=True)
-
         offsets = held.tile([P, STEPS // OFFSETS_PER_COLUMN], U16, name="offsets")
         nc.sync.dma_start(offsets[:], offs)
         table_sb = held.tile([D, NODES], BF16, name="table_sb")

@@ -30,7 +30,7 @@ def tile_autoregressivedecoder_kernel(tc, table, w, vals, lkeys, offs, out):
     nc = tc.nc
     with (
         tc.tile_pool(name="held", bufs=1) as held,
-        tc.tile_pool(name="work", bufs=NCHUNK) as work,
+        tc.tile_pool(name="work", bufs=max(NCHUNK, NB)) as work,
         tc.psum_pool(name="psum_wide", bufs=3) as psum_wide,
         tc.psum_pool(name="psum_narrow", bufs=2) as psum_narrow,
         tc.psum_pool(name="psum_held", bufs=1) as psum_held,
@@ -42,7 +42,7 @@ def tile_autoregressivedecoder_kernel(tc, table, w, vals, lkeys, offs, out):
         keys_sb = held.tile([D, NODES], BF16, name="keys_sb")
         nc.sync.dma_start(keys_sb[:], w)
         values_sb = held.tile([P, NB, D + ONES_PAD], BF16, name="values_sb")
-        nc.sync.dma_start(values_sb[:, :, 0:D], vals.rearrange("(b p) d -> p b d", p=P))
+        nc.sync.dma_start(values_sb[:, :, 0:D], vals.rearrange("(b n) d -> n b d", n=P))
         nc.vector.memset(values_sb[:, :, D : D + ONES_PAD], 1.0)
         pointer_sb = held.tile([D, NODES], BF16, name="pointer_sb")
         nc.scalar.dma_start(pointer_sb[:], lkeys)
@@ -54,12 +54,12 @@ def tile_autoregressivedecoder_kernel(tc, table, w, vals, lkeys, offs, out):
         ones_f32 = held.tile([P, P], F32, name="ones_f32")
         nc.vector.memset(ones_f32[:], 1.0)
 
+        weights = [work.tile([P, NB, CHUNK], BF16, name="weights") for c in range(NCHUNK)]
+        glimpse = [work.tile([D, CHUNK], BF16, name="glimpse") for c in range(NCHUNK)]
         clipped = held.tile([P, NCHUNK, NB, CHUNK], F32, name="clipped")
         expsum = psum_held.tile([P, NCHUNK, CHUNK], F32, name="expsum")
         logsum = held.tile([P, NCHUNK, CHUNK], F32, name="logsum")
 
-        weights = [work.tile([P, NB, CHUNK], BF16, name="weights") for c in range(NCHUNK)]
-        glimpse = [work.tile([D, CHUNK], BF16, name="glimpse") for c in range(NCHUNK)]
 
         for c in range(NCHUNK):
             scores = psum_wide.tile([P, NB, CHUNK], F32, name="scores", tag="wide")
@@ -73,11 +73,11 @@ def tile_autoregressivedecoder_kernel(tc, table, w, vals, lkeys, offs, out):
             )
             scores_sb = work.tile([P, NB, CHUNK], F32, name="scores_sb")
             nc.scalar.copy(scores_sb[:], scores[:])
-            block_top_t = psum_narrow.tile([CHUNK, P], F32, name="block_top_t", tag="narrow_a")
+            block_top_t = psum_narrow.tile([CHUNK, P], F32, name="block_top_t", tag="by_step")
             nc.tensor.transpose(block_top_t[:], block_top[:], ident_f32[:])
             top = work.tile([CHUNK, 1], F32, name="top")
             nc.vector.reduce_max(out=top[:], in_=block_top_t[:], axis=AXIS.X)
-            top_row = psum_narrow.tile([P, CHUNK], F32, name="top_row", tag="narrow_b")
+            top_row = psum_narrow.tile([P, CHUNK], F32, name="top_row", tag="turned_back")
             nc.tensor.transpose(top_row[:], top[:, 0:1].to_broadcast([CHUNK, P]), ident_f32[:])
 
             shifted = work.tile([P, NB, CHUNK], F32, name="shifted")
@@ -90,7 +90,7 @@ def tile_autoregressivedecoder_kernel(tc, table, w, vals, lkeys, offs, out):
             nc.scalar.activation(out=weights[c][:], in_=shifted[:], func=FUNC.Exp, scale=1.0 / math.sqrt(D))
 
         for c in range(NCHUNK):
-            glimpse_t = psum_narrow.tile([CHUNK, D + 1], F32, name="glimpse_t", tag="narrow_a")
+            glimpse_t = psum_narrow.tile([CHUNK, D + 1], F32, name="glimpse_t", tag="by_step")
             for b in range(NB):
                 nc.tensor.matmul(
                     glimpse_t[:], weights[c][:, b, :], values_sb[:, b, 0 : D + 1], start=(b == 0), stop=(b == NB - 1)
@@ -101,14 +101,16 @@ def tile_autoregressivedecoder_kernel(tc, table, w, vals, lkeys, offs, out):
             nc.vector.tensor_scalar(
                 out=glimpse_rows[:], in0=glimpse_t[:, 0:D], scalar1=inv_sum[:, 0:1], scalar2=None, op0=ALU.mult
             )
-            glimpse_ps = psum_narrow.tile([D, CHUNK], BF16, name="glimpse_ps", tag="narrow_b")
+            glimpse_ps = psum_narrow.tile([D, CHUNK], BF16, name="glimpse_ps", tag="turned_back")
             nc.tensor.transpose(glimpse_ps[:], glimpse_rows[:], ident_bf16[:])
             nc.vector.tensor_copy(glimpse[c][:], glimpse_ps[:])
 
         for c in range(NCHUNK):
             logits = psum_wide.tile([P, NB, CHUNK], F32, name="logits", tag="wide")
             for b in range(NB):
-                nc.tensor.matmul(logits[:, b, :], pointer_sb[:, b * P : (b + 1) * P], glimpse[c][:], start=True, stop=True)
+                nc.tensor.matmul(
+                    logits[:, b, :], pointer_sb[:, b * P : (b + 1) * P], glimpse[c][:], start=True, stop=True
+                )
             nc.scalar.activation(
                 out=clipped[:, c], in_=logits[:], func=FUNC.Tanh, scale=1.0 / math.sqrt(POINTER_DIM)
             )

import math

import concourse.mybir as mybir
from concourse.masks import make_identity

BF16 = mybir.dt.bfloat16
F32 = mybir.dt.float32
U16 = mybir.dt.uint16
FUNC = mybir.ActivationFunctionType
ALU = mybir.AluOpType
AXIS = mybir.AxisListType

P = 128
D = 128
NODES = 512
STEPS = 512
POINTER_DIM = 512
TANH_CLIP = 10.0
NB = NODES // P
CHUNK = 128
NCHUNK = STEPS // CHUNK
OFFSETS_PER_COLUMN = 16
CHUNK_COLUMNS = CHUNK // OFFSETS_PER_COLUMN
ONES_PAD = 16

FLOPS = 3 * 2 * D * NODES * STEPS


def tile_autoregressivedecoder_kernel(tc, table, w, vals, lkeys, offs, out):
    nc = tc.nc
    with (
        tc.tile_pool(name="held", bufs=1) as held,
        tc.tile_pool(name="work", bufs=max(NCHUNK, NB)) as work,
        tc.psum_pool(name="psum_wide", bufs=3) as psum_wide,
        tc.psum_pool(name="psum_narrow", bufs=2) as psum_narrow,
        tc.psum_pool(name="psum_held", bufs=1) as psum_held,
    ):
        offsets = held.tile([P, STEPS // OFFSETS_PER_COLUMN], U16, name="offsets")
        nc.sync.dma_start(offsets[:], offs)
        table_sb = held.tile([D, NODES], BF16, name="table_sb")
        nc.scalar.dma_start(table_sb[:], table)
        keys_sb = held.tile([D, NODES], BF16, name="keys_sb")
        nc.sync.dma_start(keys_sb[:], w)
        values_sb = held.tile([P, NB, D + ONES_PAD], BF16, name="values_sb")
        nc.sync.dma_start(values_sb[:, :, 0:D], vals.rearrange("(b n) d -> n b d", n=P))
        nc.vector.memset(values_sb[:, :, D : D + ONES_PAD], 1.0)
        pointer_sb = held.tile([D, NODES], BF16, name="pointer_sb")
        nc.scalar.dma_start(pointer_sb[:], lkeys)

        ident_f32 = held.tile([P, P], F32, name="ident_f32")
        make_identity(nc, ident_f32[:])
        ident_bf16 = held.tile([P, P], BF16, name="ident_bf16")
        make_identity(nc, ident_bf16[:])
        ones_f32 = held.tile([P, P], F32, name="ones_f32")
        nc.vector.memset(ones_f32[:], 1.0)

        weights = [work.tile([P, NB, CHUNK], BF16, name="weights") for c in range(NCHUNK)]
        glimpse = [work.tile([D, CHUNK], BF16, name="glimpse") for c in range(NCHUNK)]
        clipped = held.tile([P, NCHUNK, NB, CHUNK], F32, name="clipped")
        expsum = psum_held.tile([P, NCHUNK, CHUNK], F32, name="expsum")
        logsum = held.tile([P, NCHUNK, CHUNK], F32, name="logsum")


        for c in range(NCHUNK):
            scores = psum_wide.tile([P, NB, CHUNK], F32, name="scores", tag="wide")
            picked = table_sb[:].indirect(offsets[:, c * CHUNK_COLUMNS : (c + 1) * CHUNK_COLUMNS])
            for b in range(NB):
                nc.tensor.matmul(scores[:, b, :], keys_sb[:, b * P : (b + 1) * P], picked, start=True, stop=True)

            block_top = work.tile([P, CHUNK], F32, name="block_top")
            nc.vector.tensor_reduce(
                out=block_top[:], in_=scores[:].rearrange("n b j -> n j b"), axis=AXIS.X, op=ALU.max
            )
            scores_sb = work.tile([P, NB, CHUNK], F32, name="scores_sb")
            nc.scalar.copy(scores_sb[:], scores[:])
            block_top_t = psum_narrow.tile([CHUNK, P], F32, name="block_top_t", tag="by_step")
            nc.tensor.transpose(block_top_t[:], block_top[:], ident_f32[:])
            top = work.tile([CHUNK, 1], F32, name="top")
            nc.vector.reduce_max(out=top[:], in_=block_top_t[:], axis=AXIS.X)
            top_row = psum_narrow.tile([P, CHUNK], F32, name="top_row", tag="turned_back")
            nc.tensor.transpose(top_row[:], top[:, 0:1].to_broadcast([CHUNK, P]), ident_f32[:])

            shifted = work.tile([P, NB, CHUNK], F32, name="shifted")
            nc.vector.tensor_tensor(
                out=shifted[:],
                in0=scores_sb[:],
                in1=top_row[:].unsqueeze(1).to_broadcast([P, NB, CHUNK]),
                op=ALU.subtract,
            )
            nc.scalar.activation(out=weights[c][:], in_=shifted[:], func=FUNC.Exp, scale=1.0 / math.sqrt(D))

        for c in range(NCHUNK):
            glimpse_t = psum_narrow.tile([CHUNK, D + 1], F32, name="glimpse_t", tag="by_step")
            for b in range(NB):
                nc.tensor.matmul(
                    glimpse_t[:], weights[c][:, b, :], values_sb[:, b, 0 : D + 1], start=(b == 0), stop=(b == NB - 1)
                )
            inv_sum = work.tile([CHUNK, 1], F32, name="inv_sum")
            nc.vector.reciprocal(inv_sum[:], glimpse_t[:, D : D + 1])
            glimpse_rows = work.tile([CHUNK, D], BF16, name="glimpse_rows")
            nc.vector.tensor_scalar(
                out=glimpse_rows[:], in0=glimpse_t[:, 0:D], scalar1=inv_sum[:, 0:1], scalar2=None, op0=ALU.mult
            )
            glimpse_ps = psum_narrow.tile([D, CHUNK], BF16, name="glimpse_ps", tag="turned_back")
            nc.tensor.transpose(glimpse_ps[:], glimpse_rows[:], ident_bf16[:])
            nc.vector.tensor_copy(glimpse[c][:], glimpse_ps[:])

        for c in range(NCHUNK):
            logits = psum_wide.tile([P, NB, CHUNK], F32, name="logits", tag="wide")
            for b in range(NB):
                nc.tensor.matmul(
                    logits[:, b, :], pointer_sb[:, b * P : (b + 1) * P], glimpse[c][:], start=True, stop=True
                )
            nc.scalar.activation(
                out=clipped[:, c], in_=logits[:], func=FUNC.Tanh, scale=1.0 / math.sqrt(POINTER_DIM)
            )
            grown = work.tile([P, NB, CHUNK], F32, name="grown")
            nc.scalar.activation(out=grown[:], in_=clipped[:, c], func=FUNC.Exp, scale=TANH_CLIP)
            block_sum = work.tile([P, CHUNK], F32, name="block_sum")
            nc.vector.tensor_reduce(
                out=block_sum[:], in_=grown[:].rearrange("n b j -> n j b"), axis=AXIS.X, op=ALU.add
            )
            nc.tensor.matmul(expsum[:, c, :], ones_f32[:], block_sum[:], start=True, stop=True)

        nc.scalar.activation(out=logsum[:], in_=expsum[:], func=FUNC.Ln)
        for b in range(NB):
            logprob = work.tile([P, NCHUNK, CHUNK], F32, name="logprob")
            nc.vector.scalar_tensor_tensor(
                out=logprob[:],
                in0=clipped[:, :, b, :],
                scalar=TANH_CLIP,
                in1=logsum[:],
                op0=ALU.mult,
                op1=ALU.subtract,
            )
            queue = nc.sync if b % 2 == 0 else nc.scalar
            queue.dma_start(out[b * P : (b + 1) * P, :], logprob[:].rearrange("n c j -> n (c j)"))
